import numpy as np
import ml_dtypes


def mxq(x, axis, fmt="e4m3"):
    dtype, down = {"e4m3": (ml_dtypes.float8_e4m3fn, 7), "e5m2": (ml_dtypes.float8_e5m2, 14)}[fmt]
    v = np.moveaxis(np.asarray(x, np.float32).astype(ml_dtypes.bfloat16).astype(np.float64), axis, -1)
    blocks = v.reshape(v.shape[:-1] + (-1, 32))
    amax = np.abs(blocks).max(-1, keepdims=True)
    byte = np.maximum(np.where(amax > 0, np.frexp(amax)[1] - 1 + 127, 0) - down, 1)
    scale = np.exp2(byte - 127.0)
    codes = (blocks / scale).astype(np.float32).astype(dtype).astype(np.float64)
    return np.moveaxis((codes * scale).reshape(v.shape), -1, axis)


WIDE = False


def mx_kscale(k):
    if not WIDE:
        return np.ones(k)
    levels = np.array([10, -10, 5, -5, 0])
    if k % 512:
        return np.exp2(np.random.permutation(np.resize(levels, k // 32))).repeat(32)
    a = np.empty((k // 512, 16))
    for p in range(k // 512):
        a[p, :8] = np.random.permutation(np.resize(levels, 8))
        for g in range(8):
            far = levels[np.abs(levels - a[p, g]) >= 10]
            a[p, g + 8] = far[np.random.randint(len(far))]
    return np.exp2(a.ravel()).repeat(32)


BF16 = ml_dtypes.bfloat16


def bf(x):
    return np.asarray(x, np.float32).astype(BF16)


def f64(x):
    return np.asarray(x).astype(np.float64)


B, NI, NK, NJ, C_Z, C_H = 1, 4096, 512, 256, 128, 4
EPS = 1e-5
KEEP = 0.85


def layer_norm(x, w, b):
    mu = x.mean(-1, keepdims=True)
    var = ((x - mu) ** 2).mean(-1, keepdims=True)
    return (x - mu) / np.sqrt(var + EPS) * w + b


def setup_inputs():
    s = mx_kscale(NK)
    return {"a_gated": bf(np.random.standard_normal((B, NI, NK, C_H)) * 0.55 * s[None, None, :, None]),
            "b_gated": bf(np.random.standard_normal((B, NK, NJ, C_H)) * 0.55 / s[None, :, None, None]),
            "mask_ik": bf(np.random.random((B, NI, NK)) < KEEP),
            "mask_kj": bf(np.random.random((B, NK, NJ)) < KEEP),
            "ln_out_w": bf(1.0 + 0.1 * np.random.standard_normal(C_H)),
            "ln_out_b": bf(0.1 * np.random.standard_normal(C_H))}


def reference(a_gated, b_gated, mask_ik, mask_kj, ln_out_w, ln_out_b):
    a = f64(mask_ik)[..., None] * f64(a_gated)
    b = f64(mask_kj)[..., None] * f64(b_gated)
    at = a.transpose(0, 3, 1, 2)
    bt = b.transpose(0, 3, 1, 2)
    x = (mxq(at, 3, "e4m3") @ mxq(bt, 2, "e4m3")).transpose(0, 2, 3, 1)
    return layer_norm(x, f64(ln_out_w), f64(ln_out_b))

@@ -1,0 +1,223 @@
+from contextlib import ExitStack
+
+import concourse.mybir as mybir
+from concourse.masks import make_identity
+
+BF16 = mybir.dt.bfloat16
+F32 = mybir.dt.float32
+U32 = mybir.dt.uint32
+U8 = mybir.dt.uint8
+FP8X4 = mybir.dt.float8_e4m3fn_x4
+ALU = mybir.AluOpType
+ACT = mybir.ActivationFunctionType
+
+NI, NK, NJ, ND = 4096, 512, 256, 4
+EPS = 1e-5
+FLOPS = 2 * NI * NK * NJ * ND
+
+P = 128
+PACK = 4
+I_TILE = P
+TILES = 2
+ROUND = TILES * I_TILE
+ROUNDS = NI // ROUND
+GROUPED = I_TILE * PACK
+
+PAIR_SIGN = (1.0, -1.0, 1.0, -1.0)
+HALF_SIGN = (1.0, 1.0, -1.0, -1.0)
+PLUS, MINUS = 0, 1
+
+
+def tile_trianglemultiplicativeupdate_pa_t_kernel(
+    tc, a_gated, b_gated, mask_ik, mask_kj, ln_out_w, ln_out_b, out
+):
+    nc = tc.nc
+    with ExitStack() as ctx:
+        keep = ctx.enter_context(tc.tile_pool(name="keep", bufs=1))
+        loads = ctx.enter_context(tc.tile_pool(name="loads", bufs=3))
+        front = ctx.enter_context(tc.tile_pool(name="front", bufs=2))
+        norm = ctx.enter_context(tc.tile_pool(name="norm", bufs=2))
+        flipped = ctx.enter_context(tc.psum_pool(name="flipped", bufs=2))
+        sums = ctx.enter_context(tc.psum_pool(name="sums", bufs=2))
+
+        a_rounds = a_gated[0].rearrange("(r h p) k d -> r p h (k d)", h=TILES, p=P)
+        m_rounds = mask_ik[0].rearrange("(r h p) k -> r p h k", h=TILES, p=P)
+        out_tiles = out[0].rearrange("(r h p) j d -> r h p (j d)", h=TILES, p=P)
+
+        identity = keep.tile([P, P], BF16)
+        make_identity(nc, identity[:])
+
+        def load_round(r):
+            a_raw = loads.tile([P, TILES, NK * ND], BF16)
+            nc.sync.dma_start(out=a_raw[:], in_=a_rounds[r])
+            m_raw = loads.tile([P, TILES, NK], BF16)
+            nc.sync.dma_start(out=m_raw[:], in_=m_rounds[r])
+            return a_raw, m_raw
+
+        first_raw = load_round(0)
+
+        b_raw = keep.tile([P, PACK, NJ * ND], BF16)
+        nc.sync.dma_start(out=b_raw[:], in_=b_gated[0].rearrange("(q t) j d -> q t (j d)", t=PACK))
+        mkj = keep.tile([P, PACK, NJ], BF16)
+        nc.sync.dma_start(out=mkj[:], in_=mask_kj[0].rearrange("(q t) j -> q t j", t=PACK))
+        w_rows = keep.tile([P, ND], BF16)
+        nc.sync.dma_start(out=w_rows[:], in_=ln_out_w.partition_broadcast(P))
+        bias_rows = keep.tile([P, ND], BF16)
+        nc.sync.dma_start(out=bias_rows[:], in_=ln_out_b.partition_broadcast(P))
+
+        b_grouped = keep.tile([P, 2, ND, NJ * PACK], BF16, align_bytes=64)
+        for d in range(ND):
+            nc.vector.tensor_tensor(
+                out=b_grouped[:, PLUS, d, :].rearrange("p (j t) -> p j t", t=PACK),
+                in0=b_raw[:].rearrange("p t (j d) -> p d j t", d=ND)[:, d],
+                in1=mkj[:].rearrange("p t j -> p j t"),
+                op=ALU.mult,
+            )
+        nc.vector.tensor_scalar_mul(
+            out=b_grouped[:, MINUS].rearrange("p d c -> p (d c)"),
+            in0=b_grouped[:, PLUS].rearrange("p d c -> p (d c)"),
+            scalar1=-1.0,
+        )
+        b_codes = keep.tile([P, 2, ND, NJ], U32, align_bytes=64)
+        b_scales = keep.tile([P, 2, ND, NJ], U8, align_bytes=64)
+        for sign in (PLUS, MINUS):
+            nc.vector.quantize_mx(
+                out=b_codes[:, sign].rearrange("p d j -> p (d j)").bitcast(FP8X4),
+                scales=b_scales[:, sign].rearrange("p d j -> p (d j)"),
+                in_=b_grouped[:, sign].rearrange("p d c -> p (d c)"),
+            )
+
+        pair_gain = keep.tile([P, ND], F32)
+        half_gain = keep.tile([P, ND], F32)
+        shift = keep.tile([P, ND], F32)
+        for d in range(ND):
+            nc.vector.tensor_scalar_mul(
+                out=pair_gain[:, d : d + 1], in0=w_rows[:, d : d + 1], scalar1=PAIR_SIGN[d]
+            )
+            nc.vector.tensor_scalar_mul(
+                out=half_gain[:, d : d + 1], in0=w_rows[:, d : d + 1], scalar1=HALF_SIGN[d]
+            )
+        nc.vector.tensor_copy(out=shift[:], in_=bias_rows[:])
+
+        def quantise_round(r):
+            a_raw, m_raw = load_round(r) if r > 0 else first_raw
+
+            m_by_t = m_raw[:].rearrange("p h (q t) -> p h t q", t=PACK)
+            m_flip = flipped.tile([P, TILES, PACK, I_TILE], BF16, tag="flip")
+            for h in range(TILES):
+                for t in range(PACK):
+                    nc.tensor.transpose(m_flip[:, h, t, :], m_by_t[:, h, t, :], identity[:])
+            m_grouped = front.tile([P, TILES, GROUPED], BF16)
+            nc.scalar.copy(
+                out=m_grouped[:].rearrange("p h (i t) -> p h i t", t=PACK),
+                in_=m_flip[:].rearrange("p h t i -> p h i t"),
+            )
+
+            a_by_channel = a_raw[:].rearrange("p h (q t d) -> p h d t q", t=PACK, d=ND)
+            a_grouped = front.tile([P, TILES, ND, GROUPED], BF16, align_bytes=64)
+            a_codes = front.tile([P, TILES, ND, I_TILE], U32, align_bytes=64)
+            a_scales = front.tile([P, TILES, ND, I_TILE], U8, align_bytes=64)
+            for h in range(TILES):
+                for pair in range(ND // 2):
+                    a_flip = flipped.tile([P, 2, PACK, I_TILE], BF16, tag="flip")
+                    for e in range(2):
+                        for t in range(PACK):
+                            nc.tensor.transpose(
+                                a_flip[:, e, t, :], a_by_channel[:, h, 2 * pair + e, t, :], identity[:]
+                            )
+                    for e in range(2):
+                        nc.vector.tensor_tensor(
+                            out=a_grouped[:, h, 2 * pair + e, :].rearrange("p (i t) -> p i t", t=PACK),
+                            in0=a_flip[:, e].rearrange("p t i -> p i t"),
+                            in1=m_grouped[:, h, :].rearrange("p (i t) -> p i t", t=PACK),
+                            op=ALU.mult,
+                        )
+                nc.vector.quantize_mx(
+                    out=a_codes[:, h].rearrange("p d i -> p (d i)").bitcast(FP8X4),
+                    scales=a_scales[:, h].rearrange("p d i -> p (d i)"),
+                    in_=a_grouped[:, h].rearrange("p d c -> p (d c)"),
+                )
+            return a_codes, a_scales
+
+        def multiply_and_normalise(r, a_codes, a_scales):
+            c1 = sums.tile([P, TILES, NJ], F32)
+            c2 = sums.tile([P, TILES, NJ], F32)
+            c3 = sums.tile([P, TILES, NJ], F32)
+            pair_sums = (c1, c2)
+
+            def mx_pass(acc, h, d, sign, start, stop):
+                nc.tensor.matmul_mx(
+                    out=acc[:, h, :],
+                    lhsT=a_codes[:, h, d, :].bitcast(FP8X4),
+                    lhsT_scale=a_scales[:, h, d, :],
+                    rhs=b_codes[:, sign, d, :].bitcast(FP8X4),
+                    rhs_scale=b_scales[:, sign, d, :],
+                    start=start,
+                    stop=stop,
+                )
+
+            for h in range(TILES):
+                for d in range(ND):
+                    mx_pass(pair_sums[d // 2], h, d, PLUS if PAIR_SIGN[d] > 0 else MINUS,
+                            d % 2 == 0, d % 2 == 1)
+                    mx_pass(c3, h, d, PLUS if HALF_SIGN[d] > 0 else MINUS, d == 0, d == ND - 1)
+
+            wide = TILES * NJ
+            squares = norm.tile([P, 3, wide], F32)
+            for n, c in enumerate((c1, c2, c3)):
+                nc.scalar.square(out=squares[:, n, :], in_=c[:].rearrange("p h j -> p (h j)"))
+            pair_squares = norm.tile([P, wide], F32)
+            nc.vector.tensor_tensor(
+                out=pair_squares[:], in0=squares[:, 0, :], in1=squares[:, 1, :], op=ALU.add
+            )
+            var16 = norm.tile([P, wide], F32)
+            nc.vector.scalar_tensor_tensor(
+                out=var16[:], in0=pair_squares[:], scalar=2.0, in1=squares[:, 2, :],
+                op0=ALU.mult, op1=ALU.add,
+            )
+            rstd = norm.tile([P, wide], F32)
+            nc.scalar.activation(
+                out=rstd[:], in_=var16[:], func=ACT.Abs_reciprocal_sqrt, scale=1.0 / 16.0, bias=EPS
+            )
+            pair_norm = norm.tile([P, 2, wide], F32)
+            for n in range(2):
+                nc.vector.scalar_tensor_tensor(
+                    out=pair_norm[:, n, :],
+                    in0=pair_sums[n][:].rearrange("p h j -> p (h j)"),
+                    scalar=0.5,
+                    in1=rstd[:],
+                    op0=ALU.mult,
+                    op1=ALU.mult,
+                )
+            pair_part = norm.tile([P, ND, wide], F32)
+            for d in range(ND):
+                nc.scalar.activation(
+                    out=pair_part[:, d, :], in_=pair_norm[:, d // 2, :], func=ACT.Identity,
+                    scale=pair_gain[:, d : d + 1],
+                )
+            half_norm = norm.tile([P, wide], F32)
+            nc.vector.scalar_tensor_tensor(
+                out=half_norm[:], in0=c3[:].rearrange("p h j -> p (h j)"), scalar=0.25,
+                in1=rstd[:], op0=ALU.mult, op1=ALU.mult,
+            )
+            half_part = norm.tile([P, ND, wide], F32)
+            for d in range(ND):
+                nc.scalar.activation(
+                    out=half_part[:, d, :], in_=half_norm[:], func=ACT.Identity,
+                    scale=half_gain[:, d : d + 1], bias=shift[:, d : d + 1],
+                )
+            y = norm.tile([P, TILES, NJ * ND], F32)
+            for h, engine in enumerate((nc.gpsimd, nc.vector)):
+                engine.tensor_tensor(
+                    out=y[:, h, :].rearrange("p (g n d) -> p g d n", n=2, d=ND),
+                    in0=pair_part[:, :, h * NJ : (h + 1) * NJ].rearrange("p d (g n) -> p g d n", n=2),
+                    in1=half_part[:, :, h * NJ : (h + 1) * NJ].rearrange("p d (g n) -> p g d n", n=2),
+                    op=ALU.add,
+                )
+                nc.sync.dma_start(out=out_tiles[r, h], in_=y[:, h, :])
+
+        ready = quantise_round(0)
+        for r in range(ROUNDS):
+            following = quantise_round(r + 1) if r + 1 < ROUNDS else None
+            multiply_and_normalise(r, ready[0], ready[1])
+            ready = following

@@ -44,7 +44,7 @@ def tile_trianglemultiplicativeupdate_pa_t_kernel(
         m_rounds = mask_ik[0].rearrange("(r h p) k -> r p h k", h=TILES, p=P)
         out_tiles = out[0].rearrange("(r h p) j d -> r h p (j d)", h=TILES, p=P)
 
-        identity = keep.tile([P, P], BF16)
+        identity = keep.tile([P, P], F32)
         make_identity(nc, identity[:])
 
         def load_round(r):
@@ -102,36 +102,40 @@ def tile_trianglemultiplicativeupdate_pa_t_kernel(
         def quantise_round(r):
             a_raw, m_raw = load_round(r) if r > 0 else first_raw
 
-            m_by_t = m_raw[:].rearrange("p h (q t) -> p h t q", t=PACK)
-            m_flip = flipped.tile([P, TILES, PACK, I_TILE], BF16, tag="flip")
+            m_words = m_raw[:].rearrange("p h k -> p (h k)").bitcast(F32)
+            m_by_u = m_words.rearrange("p (h q u) -> p h u q", h=TILES, u=PACK // 2)
+            m_flip = flipped.tile([P, TILES, PACK // 2, I_TILE], F32, tag="flip")
             for h in range(TILES):
-                for t in range(PACK):
-                    nc.tensor.transpose(m_flip[:, h, t, :], m_by_t[:, h, t, :], identity[:])
+                for u in range(PACK // 2):
+                    nc.tensor.transpose(m_flip[:, h, u, :], m_by_u[:, h, u, :], identity[:])
             m_grouped = front.tile([P, TILES, GROUPED], BF16)
             nc.scalar.copy(
-                out=m_grouped[:].rearrange("p h (i t) -> p h i t", t=PACK),
-                in_=m_flip[:].rearrange("p h t i -> p h i t"),
+                out=m_grouped[:].rearrange("p h c -> p (h c)").bitcast(F32).rearrange(
+                    "p (h i u) -> p h i u", h=TILES, u=PACK // 2
+                ),
+                in_=m_flip[:].rearrange("p h u i -> p h i u"),
             )
 
-            a_by_channel = a_raw[:].rearrange("p h (q t d) -> p h d t q", t=PACK, d=ND)
+            a_words = a_raw[:].rearrange("p h c -> p (h c)").bitcast(F32)
+            a_by_pair = a_words.rearrange("p (h q t n) -> p h n t q", h=TILES, t=PACK, n=ND // 2)
             a_grouped = front.tile([P, TILES, ND, GROUPED], BF16, align_bytes=64)
             a_codes = front.tile([P, TILES, ND, I_TILE], U32, align_bytes=64)
             a_scales = front.tile([P, TILES, ND, I_TILE], U8, align_bytes=64)
             for h in range(TILES):
                 for pair in range(ND // 2):
-                    a_flip = flipped.tile([P, 2, PACK, I_TILE], BF16, tag="flip")
-                    for e in range(2):
-                        for t in range(PACK):
-                            nc.tensor.transpose(
-                                a_flip[:, e, t, :], a_by_channel[:, h, 2 * pair + e, t, :], identity[:]
-                            )
-                    for e in range(2):
-                        nc.vector.tensor_tensor(
-                            out=a_grouped[:, h, 2 * pair + e, :].rearrange("p (i t) -> p i t", t=PACK),
-                            in0=a_flip[:, e].rearrange("p t i -> p i t"),
-                            in1=m_grouped[:, h, :].rearrange("p (i t) -> p i t", t=PACK),
-                            op=ALU.mult,
+                    a_flip = flipped.tile([P, PACK * I_TILE], F32, tag="flip")
+                    for t in range(PACK):
+                        nc.tensor.transpose(
+                            a_flip[:, t * I_TILE : (t + 1) * I_TILE], a_by_pair[:, h, pair, t, :], identity[:]
                         )
+                    nc.vector.tensor_tensor(
+                        out=a_grouped[:, h, 2 * pair : 2 * pair + 2, :].rearrange("p e (i t) -> p e i t", t=PACK),
+                        in0=a_flip[:].bitcast(BF16).rearrange("p (t i e) -> p e i t", t=PACK, e=2),
+                        in1=m_grouped[:, h, :].rearrange("p (i t) -> p i t", t=PACK).unsqueeze(1).to_broadcast(
+                            [P, 2, I_TILE, PACK]
+                        ),
+                        op=ALU.mult,
+                    )
                 nc.vector.quantize_mx(
                     out=a_codes[:, h].rearrange("p d i -> p (d i)").bitcast(FP8X4),
                     scales=a_scales[:, h].rearrange("p d i -> p (d i)"),

@@ -1,3 +1,4 @@
+import math
 from contextlib import ExitStack
 
 import concourse.mybir as mybir
@@ -25,6 +26,7 @@ GROUPED = I_TILE * PACK
 
 PAIR_SIGN = (1.0, -1.0, 1.0, -1.0)
 HALF_SIGN = (1.0, 1.0, -1.0, -1.0)
+SHARE = (math.sqrt(1 / 8), math.sqrt(1 / 8), 1 / 4)
 PLUS, MINUS = 0, 1
 
 
@@ -37,8 +39,8 @@ def tile_trianglemultiplicativeupdate_pa_t_kernel(
         loads = ctx.enter_context(tc.tile_pool(name="loads", bufs=3))
         front = ctx.enter_context(tc.tile_pool(name="front", bufs=2))
         norm = ctx.enter_context(tc.tile_pool(name="norm", bufs=2))
-        flipped = ctx.enter_context(tc.psum_pool(name="flipped", bufs=2))
-        sums = ctx.enter_context(tc.psum_pool(name="sums", bufs=2))
+        flipped = ctx.enter_context(tc.psum_pool(name="flipped", bufs=3))
+        sums = ctx.enter_context(tc.psum_pool(name="sums", bufs=5))
 
         a_rounds = a_gated[0].rearrange("(r h p) k d -> r p h (k d)", h=TILES, p=P)
         m_rounds = mask_ik[0].rearrange("(r h p) k -> r p h k", h=TILES, p=P)
@@ -136,17 +138,17 @@ def tile_trianglemultiplicativeupdate_pa_t_kernel(
                         ),
                         op=ALU.mult,
                     )
-                nc.vector.quantize_mx(
-                    out=a_codes[:, h].rearrange("p d i -> p (d i)").bitcast(FP8X4),
-                    scales=a_scales[:, h].rearrange("p d i -> p (d i)"),
-                    in_=a_grouped[:, h].rearrange("p d c -> p (d c)"),
-                )
+            nc.vector.quantize_mx(
+                out=a_codes[:].rearrange("p h d i -> p (h d i)").bitcast(FP8X4),
+                scales=a_scales[:].rearrange("p h d i -> p (h d i)"),
+                in_=a_grouped[:].rearrange("p h d c -> p (h d c)"),
+            )
             return a_codes, a_scales
 
         def multiply_and_normalise(r, a_codes, a_scales):
-            c1 = sums.tile([P, TILES, NJ], F32)
-            c2 = sums.tile([P, TILES, NJ], F32)
-            c3 = sums.tile([P, TILES, NJ], F32)
+            c1 = sums.tile([P, TILES, NJ], F32, tag="contrast")
+            c2 = sums.tile([P, TILES, NJ], F32, tag="contrast")
+            c3 = sums.tile([P, TILES, NJ], F32, tag="contrast")
             pair_sums = (c1, c2)
 
             def mx_pass(acc, h, d, sign, start, stop):
@@ -169,19 +171,19 @@ def tile_trianglemultiplicativeupdate_pa_t_kernel(
             wide = TILES * NJ
             squares = norm.tile([P, 3, wide], F32)
             for n, c in enumerate((c1, c2, c3)):
-                nc.scalar.square(out=squares[:, n, :], in_=c[:].rearrange("p h j -> p (h j)"))
+                nc.scalar.activation(
+                    out=squares[:, n, :], in_=c[:].rearrange("p h j -> p (h j)"), func=ACT.Square,
+                    scale=SHARE[n],
+                )
             pair_squares = norm.tile([P, wide], F32)
-            nc.vector.tensor_tensor(
+            nc.gpsimd.tensor_tensor(
                 out=pair_squares[:], in0=squares[:, 0, :], in1=squares[:, 1, :], op=ALU.add
             )
-            var16 = norm.tile([P, wide], F32)
-            nc.vector.scalar_tensor_tensor(
-                out=var16[:], in0=pair_squares[:], scalar=2.0, in1=squares[:, 2, :],
-                op0=ALU.mult, op1=ALU.add,
-            )
+            var = norm.tile([P, wide], F32)
+            nc.gpsimd.tensor_tensor(out=var[:], in0=pair_squares[:], in1=squares[:, 2, :], op=ALU.add)
             rstd = norm.tile([P, wide], F32)
             nc.scalar.activation(
-                out=rstd[:], in_=var16[:], func=ACT.Abs_reciprocal_sqrt, scale=1.0 / 16.0, bias=EPS
+                out=rstd[:], in_=var[:], func=ACT.Abs_reciprocal_sqrt, scale=1.0, bias=EPS
             )
             pair_norm = norm.tile([P, 2, wide], F32)
             for n in range(2):
@@ -211,8 +213,8 @@ def tile_trianglemultiplicativeupdate_pa_t_kernel(
                     scale=half_gain[:, d : d + 1], bias=shift[:, d : d + 1],
                 )
             y = norm.tile([P, TILES, NJ * ND], F32)
-            for h, engine in enumerate((nc.gpsimd, nc.vector)):
-                engine.tensor_tensor(
+            for h in range(TILES):
+                nc.gpsimd.tensor_tensor(
                     out=y[:, h, :].rearrange("p (g n d) -> p g d n", n=2, d=ND),
                     in0=pair_part[:, :, h * NJ : (h + 1) * NJ].rearrange("p d (g n) -> p g d n", n=2),
                     in1=half_part[:, :, h * NJ : (h + 1) * NJ].rearrange("p d (g n) -> p g d n", n=2),

@@ -26,6 +26,7 @@ GROUPED = I_TILE * PACK
 
 PAIR_SIGN = (1.0, -1.0, 1.0, -1.0)
 HALF_SIGN = (1.0, 1.0, -1.0, -1.0)
+FACTOR = (0.5, 0.5, 0.25)
 SHARE = (math.sqrt(1 / 8), math.sqrt(1 / 8), 1 / 4)
 PLUS, MINUS = 0, 1
 
@@ -36,11 +37,12 @@ def tile_trianglemultiplicativeupdate_pa_t_kernel(
     nc = tc.nc
     with ExitStack() as ctx:
         keep = ctx.enter_context(tc.tile_pool(name="keep", bufs=1))
-        loads = ctx.enter_context(tc.tile_pool(name="loads", bufs=3))
+        loads = ctx.enter_context(tc.tile_pool(name="loads", bufs=4))
         front = ctx.enter_context(tc.tile_pool(name="front", bufs=2))
         norm = ctx.enter_context(tc.tile_pool(name="norm", bufs=2))
         flipped = ctx.enter_context(tc.psum_pool(name="flipped", bufs=3))
-        sums = ctx.enter_context(tc.psum_pool(name="sums", bufs=5))
+        flipped_mask = ctx.enter_context(tc.psum_pool(name="flipped_mask", bufs=1))
+        sums = ctx.enter_context(tc.psum_pool(name="sums", bufs=4))
 
         a_rounds = a_gated[0].rearrange("(r h p) k d -> r p h (k d)", h=TILES, p=P)
         m_rounds = mask_ik[0].rearrange("(r h p) k -> r p h k", h=TILES, p=P)
@@ -101,129 +103,207 @@ def tile_trianglemultiplicativeupdate_pa_t_kernel(
             )
         nc.vector.tensor_copy(out=shift[:], in_=bias_rows[:])
 
-        def quantise_round(r):
-            a_raw, m_raw = load_round(r) if r > 0 else first_raw
+        WIDE = TILES * NJ
 
-            m_words = m_raw[:].rearrange("p h k -> p (h k)").bitcast(F32)
+        def flip_mask(st):
+            m_words = st["m_raw"][:].rearrange("p h k -> p (h k)").bitcast(F32)
             m_by_u = m_words.rearrange("p (h q u) -> p h u q", h=TILES, u=PACK // 2)
-            m_flip = flipped.tile([P, TILES, PACK // 2, I_TILE], F32, tag="flip")
+            m_flip = flipped_mask.tile([P, TILES, PACK // 2, I_TILE], F32)
             for h in range(TILES):
                 for u in range(PACK // 2):
                     nc.tensor.transpose(m_flip[:, h, u, :], m_by_u[:, h, u, :], identity[:])
+            st["m_flip"] = m_flip
+
+        def group_mask(st):
             m_grouped = front.tile([P, TILES, GROUPED], BF16)
             nc.scalar.copy(
                 out=m_grouped[:].rearrange("p h c -> p (h c)").bitcast(F32).rearrange(
                     "p (h i u) -> p h i u", h=TILES, u=PACK // 2
                 ),
-                in_=m_flip[:].rearrange("p h u i -> p h i u"),
+                in_=st["m_flip"][:].rearrange("p h u i -> p h i u"),
+            )
+            st["m_grouped"] = m_grouped
+
+        def flip_pair(st, part):
+            h, pair = divmod(part, ND // 2)
+            a_words = st["a_raw"][:].rearrange("p h c -> p (h c)").bitcast(F32)
+            a_by_pair = a_words.rearrange("p (h q t n) -> p h n t q", h=TILES, t=PACK, n=ND // 2)
+            a_flip = flipped.tile([P, PACK * I_TILE], F32)
+            for t in range(PACK):
+                nc.tensor.transpose(
+                    a_flip[:, t * I_TILE : (t + 1) * I_TILE], a_by_pair[:, h, pair, t, :], identity[:]
+                )
+            st["a_flip", part] = a_flip
+
+        def mask_pair(st, part):
+            h, pair = divmod(part, ND // 2)
+            if part == 0:
+                st["a_grouped"] = front.tile([P, TILES, ND, GROUPED], BF16, name="a_grouped", align_bytes=64)
+            nc.vector.tensor_tensor(
+                out=st["a_grouped"][:, h, 2 * pair : 2 * pair + 2, :].rearrange("p e (i t) -> p e i t", t=PACK),
+                in0=st["a_flip", part][:].bitcast(BF16).rearrange("p (t i e) -> p e i t", t=PACK, e=2),
+                in1=st["m_grouped"][:, h, :].rearrange("p (i t) -> p i t", t=PACK).unsqueeze(1).to_broadcast(
+                    [P, 2, I_TILE, PACK]
+                ),
+                op=ALU.mult,
             )
 
-            a_words = a_raw[:].rearrange("p h c -> p (h c)").bitcast(F32)
-            a_by_pair = a_words.rearrange("p (h q t n) -> p h n t q", h=TILES, t=PACK, n=ND // 2)
-            a_grouped = front.tile([P, TILES, ND, GROUPED], BF16, align_bytes=64)
+        def quantise(st):
             a_codes = front.tile([P, TILES, ND, I_TILE], U32, align_bytes=64)
             a_scales = front.tile([P, TILES, ND, I_TILE], U8, align_bytes=64)
-            for h in range(TILES):
-                for pair in range(ND // 2):
-                    a_flip = flipped.tile([P, PACK * I_TILE], F32, tag="flip")
-                    for t in range(PACK):
-                        nc.tensor.transpose(
-                            a_flip[:, t * I_TILE : (t + 1) * I_TILE], a_by_pair[:, h, pair, t, :], identity[:]
-                        )
-                    nc.vector.tensor_tensor(
-                        out=a_grouped[:, h, 2 * pair : 2 * pair + 2, :].rearrange("p e (i t) -> p e i t", t=PACK),
-                        in0=a_flip[:].bitcast(BF16).rearrange("p (t i e) -> p e i t", t=PACK, e=2),
-                        in1=m_grouped[:, h, :].rearrange("p (i t) -> p i t", t=PACK).unsqueeze(1).to_broadcast(
-                            [P, 2, I_TILE, PACK]
-                        ),
-                        op=ALU.mult,
-                    )
             nc.vector.quantize_mx(
                 out=a_codes[:].rearrange("p h d i -> p (h d i)").bitcast(FP8X4),
                 scales=a_scales[:].rearrange("p h d i -> p (h d i)"),
-                in_=a_grouped[:].rearrange("p h d c -> p (h d c)"),
+                in_=st["a_grouped"][:].rearrange("p h d c -> p (h d c)"),
             )
-            return a_codes, a_scales
+            st["a_codes"], st["a_scales"] = a_codes, a_scales
 
-        def multiply_and_normalise(r, a_codes, a_scales):
-            c1 = sums.tile([P, TILES, NJ], F32, tag="contrast")
-            c2 = sums.tile([P, TILES, NJ], F32, tag="contrast")
-            c3 = sums.tile([P, TILES, NJ], F32, tag="contrast")
-            pair_sums = (c1, c2)
+        def multiply(st):
+            for n, channels in enumerate(((0, 1), (2, 3), (0, 1, 2, 3))):
+                acc = sums.tile([P, TILES, NJ], F32)
+                st["c", n] = acc
+                signs = HALF_SIGN if n == 2 else PAIR_SIGN
+                for h in range(TILES):
+                    for d in channels:
+                        sign = PLUS if signs[d] > 0 else MINUS
+                        nc.tensor.matmul_mx(
+                            out=acc[:, h, :],
+                            lhsT=st["a_codes"][:, h, d, :].bitcast(FP8X4),
+                            lhsT_scale=st["a_scales"][:, h, d, :],
+                            rhs=b_codes[:, sign, d, :].bitcast(FP8X4),
+                            rhs_scale=b_scales[:, sign, d, :],
+                            start=(d == channels[0]),
+                            stop=(d == channels[-1]),
+                        )
 
-            def mx_pass(acc, h, d, sign, start, stop):
-                nc.tensor.matmul_mx(
-                    out=acc[:, h, :],
-                    lhsT=a_codes[:, h, d, :].bitcast(FP8X4),
-                    lhsT_scale=a_scales[:, h, d, :],
-                    rhs=b_codes[:, sign, d, :].bitcast(FP8X4),
-                    rhs_scale=b_scales[:, sign, d, :],
-                    start=start,
-                    stop=stop,
-                )
-
-            for h in range(TILES):
-                for d in range(ND):
-                    mx_pass(pair_sums[d // 2], h, d, PLUS if PAIR_SIGN[d] > 0 else MINUS,
-                            d % 2 == 0, d % 2 == 1)
-                    mx_pass(c3, h, d, PLUS if HALF_SIGN[d] > 0 else MINUS, d == 0, d == ND - 1)
-
-            wide = TILES * NJ
-            squares = norm.tile([P, 3, wide], F32)
-            for n, c in enumerate((c1, c2, c3)):
-                nc.scalar.activation(
-                    out=squares[:, n, :], in_=c[:].rearrange("p h j -> p (h j)"), func=ACT.Square,
-                    scale=SHARE[n],
-                )
-            pair_squares = norm.tile([P, wide], F32)
-            nc.gpsimd.tensor_tensor(
-                out=pair_squares[:], in0=squares[:, 0, :], in1=squares[:, 1, :], op=ALU.add
-            )
-            var = norm.tile([P, wide], F32)
-            nc.gpsimd.tensor_tensor(out=var[:], in0=pair_squares[:], in1=squares[:, 2, :], op=ALU.add)
-            rstd = norm.tile([P, wide], F32)
+        def square(st, n):
+            if n == 0:
+                st["squares"] = norm.tile([P, 3, WIDE], F32, name="squares")
             nc.scalar.activation(
-                out=rstd[:], in_=var[:], func=ACT.Abs_reciprocal_sqrt, scale=1.0, bias=EPS
+                out=st["squares"][:, n, :], in_=st["c", n][:].rearrange("p h j -> p (h j)"),
+                func=ACT.Square, scale=SHARE[n],
             )
-            pair_norm = norm.tile([P, 2, wide], F32)
-            for n in range(2):
-                nc.vector.scalar_tensor_tensor(
-                    out=pair_norm[:, n, :],
-                    in0=pair_sums[n][:].rearrange("p h j -> p (h j)"),
-                    scalar=0.5,
-                    in1=rstd[:],
-                    op0=ALU.mult,
-                    op1=ALU.mult,
-                )
-            pair_part = norm.tile([P, ND, wide], F32)
-            for d in range(ND):
-                nc.scalar.activation(
-                    out=pair_part[:, d, :], in_=pair_norm[:, d // 2, :], func=ACT.Identity,
-                    scale=pair_gain[:, d : d + 1],
-                )
-            half_norm = norm.tile([P, wide], F32)
-            nc.vector.scalar_tensor_tensor(
-                out=half_norm[:], in0=c3[:].rearrange("p h j -> p (h j)"), scalar=0.25,
-                in1=rstd[:], op0=ALU.mult, op1=ALU.mult,
-            )
-            half_part = norm.tile([P, ND, wide], F32)
-            for d in range(ND):
-                nc.scalar.activation(
-                    out=half_part[:, d, :], in_=half_norm[:], func=ACT.Identity,
-                    scale=half_gain[:, d : d + 1], bias=shift[:, d : d + 1],
-                )
-            y = norm.tile([P, TILES, NJ * ND], F32)
-            for h in range(TILES):
-                nc.gpsimd.tensor_tensor(
-                    out=y[:, h, :].rearrange("p (g n d) -> p g d n", n=2, d=ND),
-                    in0=pair_part[:, :, h * NJ : (h + 1) * NJ].rearrange("p d (g n) -> p g d n", n=2),
-                    in1=half_part[:, :, h * NJ : (h + 1) * NJ].rearrange("p d (g n) -> p g d n", n=2),
-                    op=ALU.add,
-                )
-                nc.sync.dma_start(out=out_tiles[r, h], in_=y[:, h, :])
 
-        ready = quantise_round(0)
-        for r in range(ROUNDS):
-            following = quantise_round(r + 1) if r + 1 < ROUNDS else None
-            multiply_and_normalise(r, ready[0], ready[1])
-            ready = following
+        def add_pair_squares(st):
+            pair_squares = norm.tile([P, WIDE], F32)
+            nc.gpsimd.tensor_tensor(
+                out=pair_squares[:], in0=st["squares"][:, 0, :], in1=st["squares"][:, 1, :], op=ALU.add
+            )
+            st["pair_squares"] = pair_squares
+
+        def add_third_square(st):
+            var = norm.tile([P, WIDE], F32)
+            nc.gpsimd.tensor_tensor(
+                out=var[:], in0=st["pair_squares"][:], in1=st["squares"][:, 2, :], op=ALU.add
+            )
+            st["var"] = var
+
+        def invert(st):
+            rstd = norm.tile([P, WIDE], F32)
+            nc.scalar.activation(
+                out=rstd[:], in_=st["var"][:], func=ACT.Abs_reciprocal_sqrt, scale=1.0, bias=EPS
+            )
+            st["rstd"] = rstd
+
+        def normalise(st):
+            normed = norm.tile([P, 3, WIDE], F32)
+            for n in range(3):
+                nc.vector.scalar_tensor_tensor(
+                    out=normed[:, n, :], in0=st["c", n][:].rearrange("p h j -> p (h j)"),
+                    scalar=FACTOR[n], in1=st["rstd"][:], op0=ALU.mult, op1=ALU.mult,
+                )
+            st["normed"] = normed
+
+        def pair_part(st, d):
+            if d == 0:
+                st["pair_part"] = norm.tile([P, ND, WIDE], F32, name="pair_part")
+            nc.scalar.activation(
+                out=st["pair_part"][:, d, :], in_=st["normed"][:, d // 2, :], func=ACT.Identity,
+                scale=pair_gain[:, d : d + 1],
+            )
+
+        def half_part(st, d):
+            if d == 0:
+                st["half_part"] = norm.tile([P, ND, WIDE], F32, name="half_part")
+            nc.scalar.activation(
+                out=st["half_part"][:, d, :], in_=st["normed"][:, 2, :], func=ACT.Identity,
+                scale=half_gain[:, d : d + 1], bias=shift[:, d : d + 1],
+            )
+
+        def finish(st, engine, h, first, count):
+            if (h, first) == (0, 0):
+                st["y"] = norm.tile([P, TILES, NJ * ND], F32, name="y")
+            cols = slice(h * NJ + first, h * NJ + first + count)
+            engine.tensor_tensor(
+                out=st["y"][:, h, first * ND : (first + count) * ND].rearrange(
+                    "p (g n d) -> p g d n", n=2, d=ND
+                ),
+                in0=st["pair_part"][:, :, cols].rearrange("p d (g n) -> p g d n", n=2),
+                in1=st["half_part"][:, :, cols].rearrange("p d (g n) -> p g d n", n=2),
+                op=ALU.add,
+            )
+
+        def store(r, st, h):
+            nc.sync.dma_start(out=out_tiles[r, h], in_=st["y"][:, h, :])
+
+        state = [{} for x in range(ROUNDS)]
+
+        def load(r):
+            if r < ROUNDS:
+                state[r]["a_raw"], state[r]["m_raw"] = load_round(r) if r > 0 else first_raw
+
+        with tc.manual_schedule():
+            for r in range(3):
+                load(r)
+            flip_mask(state[0])
+            group_mask(state[0])
+            for part in range(3):
+                flip_pair(state[0], part)
+            for s in range(ROUNDS + 3):
+                ahead, now, mid, back, end = [
+                    state[x] if 0 <= x < ROUNDS else None for x in (s + 1, s, s - 1, s - 2, s - 3)
+                ]
+                load(s + 3)
+                if mid:
+                    multiply(mid)
+                if now:
+                    flip_pair(now, 3)
+                if ahead:
+                    flip_mask(ahead)
+                if end:
+                    finish(end, nc.gpsimd, 0, 0, NJ // 2)
+                if mid:
+                    square(mid, 0)
+                    square(mid, 1)
+                    add_pair_squares(mid)
+                if back:
+                    pair_part(back, 0)
+                if mid:
+                    square(mid, 2)
+                    add_third_square(mid)
+                if back:
+                    pair_part(back, 1)
+                    pair_part(back, 2)
+                if mid:
+                    invert(mid)
+                for part in range(4):
+                    if now:
+                        mask_pair(now, part)
+                    if ahead and part < 3:
+                        flip_pair(ahead, part)
+                if ahead:
+                    group_mask(ahead)
+                if back:
+                    pair_part(back, 3)
+                    for d in range(ND):
+                        half_part(back, d)
+                if now:
+                    quantise(now)
+                if end:
+                    finish(end, nc.gpsimd, 0, NJ // 2, NJ // 2)
+                if mid:
+                    normalise(mid)
+                if end:
+                    finish(end, nc.vector, 1, 0, NJ)
+                    for h in range(TILES):
+                        store(s - 3, end, h)

@@ -124,8 +124,31 @@ def tile_trianglemultiplicativeupdate_pa_t_kernel(
             )
             st["m_grouped"] = m_grouped
 
+        def split_channels(st, h):
+            if h == 0:
+                st["a_split"] = front.tile([P, TILES, 2, NK], BF16, name="a_split")
+            k_by_half = st["a_raw"][:, h, :].rearrange("p (q u v d) -> p d u q v", u=2, v=2, d=ND)
+            for e in range(2):
+                nc.gpsimd.tensor_scalar(
+                    out=st["a_split"][:, h, e, :].rearrange("p (u q v) -> p u q v", u=2, v=2),
+                    in0=k_by_half[:, 2 + e],
+                    scalar1=1.0, scalar2=0.0, op0=ALU.mult, op1=ALU.add,
+                )
+
+        def flip_split(st, part):
+            words = st["a_split"][:].rearrange("p h e k -> p (h e k)").bitcast(F32)
+            a_flip = flipped.tile([P, PACK * I_TILE], F32, name="a_flip")
+            for eu in range(4):
+                first = (part // 2 * 4 + eu) * P
+                nc.tensor.transpose(
+                    a_flip[:, eu * I_TILE : (eu + 1) * I_TILE], words[:, first : first + P], identity[:]
+                )
+            st["a_flip", part] = a_flip
+
         def flip_pair(st, part):
             h, pair = divmod(part, ND // 2)
+            if pair == 1:
+                return flip_split(st, part)
             a_words = st["a_raw"][:].rearrange("p h c -> p (h c)").bitcast(F32)
             a_by_pair = a_words.rearrange("p (h q t n) -> p h n t q", h=TILES, t=PACK, n=ND // 2)
             a_flip = flipped.tile([P, PACK * I_TILE], F32)
@@ -139,6 +162,16 @@ def tile_trianglemultiplicativeupdate_pa_t_kernel(
             h, pair = divmod(part, ND // 2)
             if part == 0:
                 st["a_grouped"] = front.tile([P, TILES, ND, GROUPED], BF16, name="a_grouped", align_bytes=64)
+            if pair == 1:
+                nc.vector.tensor_tensor(
+                    out=st["a_grouped"][:, h, 2:4, :].rearrange("p e (i u v) -> p i e u v", u=2, v=2),
+                    in0=st["a_flip", part][:].bitcast(BF16).rearrange("p (e u i v) -> p i e u v", e=2, u=2, v=2),
+                    in1=st["m_grouped"][:, h, :].rearrange("p (i u v) -> p i u v", u=2, v=2).unsqueeze(2).to_broadcast(
+                        [P, I_TILE, 2, 2, 2]
+                    ),
+                    op=ALU.mult,
+                )
+                return
             nc.vector.tensor_tensor(
                 out=st["a_grouped"][:, h, 2 * pair : 2 * pair + 2, :].rearrange("p e (i t) -> p e i t", t=PACK),
                 in0=st["a_flip", part][:].bitcast(BF16).rearrange("p (t i e) -> p e i t", t=PACK, e=2),
@@ -255,13 +288,17 @@ def tile_trianglemultiplicativeupdate_pa_t_kernel(
         with tc.manual_schedule():
             for r in range(3):
                 load(r)
+            for h in range(TILES):
+                split_channels(state[0], h)
             flip_mask(state[0])
             group_mask(state[0])
             for part in range(3):
                 flip_pair(state[0], part)
+            for h in range(TILES):
+                split_channels(state[1], h)
             for s in range(ROUNDS + 3):
-                ahead, now, mid, back, end = [
-                    state[x] if 0 <= x < ROUNDS else None for x in (s + 1, s, s - 1, s - 2, s - 3)
+                far, ahead, now, mid, back, end = [
+                    state[x] if 0 <= x < ROUNDS else None for x in (s + 2, s + 1, s, s - 1, s - 2, s - 3)
                 ]
                 load(s + 3)
                 if mid:
@@ -270,8 +307,8 @@ def tile_trianglemultiplicativeupdate_pa_t_kernel(
                     flip_pair(now, 3)
                 if ahead:
                     flip_mask(ahead)
-                if end:
-                    finish(end, nc.gpsimd, 0, 0, NJ // 2)
+                if far:
+                    split_channels(far, 0)
                 if mid:
                     square(mid, 0)
                     square(mid, 1)
@@ -281,6 +318,8 @@ def tile_trianglemultiplicativeupdate_pa_t_kernel(
                 if mid:
                     square(mid, 2)
                     add_third_square(mid)
+                if far:
+                    split_channels(far, 1)
                 if back:
                     pair_part(back, 1)
                     pair_part(back, 2)
@@ -300,10 +339,9 @@ def tile_trianglemultiplicativeupdate_pa_t_kernel(
                 if now:
                     quantise(now)
                 if end:
-                    finish(end, nc.gpsimd, 0, NJ // 2, NJ // 2)
-                if mid:
-                    normalise(mid)
-                if end:
+                    finish(end, nc.vector, 0, 0, NJ)
                     finish(end, nc.vector, 1, 0, NJ)
                     for h in range(TILES):
                         store(s - 3, end, h)
+                if mid:
+                    normalise(mid)

@@ -307,8 +307,10 @@ def tile_trianglemultiplicativeupdate_pa_t_kernel(
                     flip_pair(now, 3)
                 if ahead:
                     flip_mask(ahead)
-                if far:
-                    split_channels(far, 0)
+                if end:
+                    for h in range(TILES):
+                        finish(end, nc.vector, h, 0, NJ)
+                        store(s - 3, end, h)
                 if mid:
                     square(mid, 0)
                     square(mid, 1)
@@ -319,7 +321,8 @@ def tile_trianglemultiplicativeupdate_pa_t_kernel(
                     square(mid, 2)
                     add_third_square(mid)
                 if far:
-                    split_channels(far, 1)
+                    for h in range(TILES):
+                        split_channels(far, h)
                 if back:
                     pair_part(back, 1)
                     pair_part(back, 2)
@@ -338,10 +341,5 @@ def tile_trianglemultiplicativeupdate_pa_t_kernel(
                         half_part(back, d)
                 if now:
                     quantise(now)
-                if end:
-                    finish(end, nc.vector, 0, 0, NJ)
-                    finish(end, nc.vector, 1, 0, NJ)
-                    for h in range(TILES):
-                        store(s - 3, end, h)
                 if mid:
                     normalise(mid)

import math
from contextlib import ExitStack

import concourse.mybir as mybir
from concourse.masks import make_identity

BF16 = mybir.dt.bfloat16
F32 = mybir.dt.float32
U32 = mybir.dt.uint32
U8 = mybir.dt.uint8
FP8X4 = mybir.dt.float8_e4m3fn_x4
ALU = mybir.AluOpType
ACT = mybir.ActivationFunctionType

NI, NK, NJ, ND = 4096, 512, 256, 4
EPS = 1e-5
FLOPS = 2 * NI * NK * NJ * ND

P = 128
PACK = 4
I_TILE = P
TILES = 2
ROUND = TILES * I_TILE
ROUNDS = NI // ROUND
GROUPED = I_TILE * PACK

PAIR_SIGN = (1.0, -1.0, 1.0, -1.0)
HALF_SIGN = (1.0, 1.0, -1.0, -1.0)
FACTOR = (0.5, 0.5, 0.25)
SHARE = (math.sqrt(1 / 8), math.sqrt(1 / 8), 1 / 4)
PLUS, MINUS = 0, 1


def tile_trianglemultiplicativeupdate_pa_t_kernel(
    tc, a_gated, b_gated, mask_ik, mask_kj, ln_out_w, ln_out_b, out
):
    nc = tc.nc
    with ExitStack() as ctx:
        keep = ctx.enter_context(tc.tile_pool(name="keep", bufs=1))
        loads = ctx.enter_context(tc.tile_pool(name="loads", bufs=4))
        front = ctx.enter_context(tc.tile_pool(name="front", bufs=2))
        norm = ctx.enter_context(tc.tile_pool(name="norm", bufs=2))
        flipped = ctx.enter_context(tc.psum_pool(name="flipped", bufs=3))
        flipped_mask = ctx.enter_context(tc.psum_pool(name="flipped_mask", bufs=1))
        sums = ctx.enter_context(tc.psum_pool(name="sums", bufs=4))

        a_rounds = a_gated[0].rearrange("(r h p) k d -> r p h (k d)", h=TILES, p=P)
        m_rounds = mask_ik[0].rearrange("(r h p) k -> r p h k", h=TILES, p=P)
        out_tiles = out[0].rearrange("(r h p) j d -> r h p (j d)", h=TILES, p=P)

        identity = keep.tile([P, P], F32)
        make_identity(nc, identity[:])

        def load_round(r):
            a_raw = loads.tile([P, TILES, NK * ND], BF16)
            nc.sync.dma_start(out=a_raw[:], in_=a_rounds[r])
            m_raw = loads.tile([P, TILES, NK], BF16)
            nc.sync.dma_start(out=m_raw[:], in_=m_rounds[r])
            return a_raw, m_raw

        first_raw = load_round(0)

        b_raw = keep.tile([P, PACK, NJ * ND], BF16)
        nc.sync.dma_start(out=b_raw[:], in_=b_gated[0].rearrange("(q t) j d -> q t (j d)", t=PACK))
        mkj = keep.tile([P, PACK, NJ], BF16)
        nc.sync.dma_start(out=mkj[:], in_=mask_kj[0].rearrange("(q t) j -> q t j", t=PACK))
        w_rows = keep.tile([P, ND], BF16)
        nc.sync.dma_start(out=w_rows[:], in_=ln_out_w.partition_broadcast(P))
        bias_rows = keep.tile([P, ND], BF16)
        nc.sync.dma_start(out=bias_rows[:], in_=ln_out_b.partition_broadcast(P))

        b_grouped = keep.tile([P, 2, ND, NJ * PACK], BF16, align_bytes=64)
        for d in range(ND):
            nc.vector.tensor_tensor(
                out=b_grouped[:, PLUS, d, :].rearrange("p (j t) -> p j t", t=PACK),
                in0=b_raw[:].rearrange("p t (j d) -> p d j t", d=ND)[:, d],
                in1=mkj[:].rearrange("p t j -> p j t"),
                op=ALU.mult,
            )
        nc.vector.tensor_scalar_mul(
            out=b_grouped[:, MINUS].rearrange("p d c -> p (d c)"),
            in0=b_grouped[:, PLUS].rearrange("p d c -> p (d c)"),
            scalar1=-1.0,
        )
        b_codes = keep.tile([P, 2, ND, NJ], U32, align_bytes=64)
        b_scales = keep.tile([P, 2, ND, NJ], U8, align_bytes=64)
        for sign in (PLUS, MINUS):
            nc.vector.quantize_mx(
                out=b_codes[:, sign].rearrange("p d j -> p (d j)").bitcast(FP8X4),
                scales=b_scales[:, sign].rearrange("p d j -> p (d j)"),
                in_=b_grouped[:, sign].rearrange("p d c -> p (d c)"),
            )

        pair_gain = keep.tile([P, ND], F32)
        half_gain = keep.tile([P, ND], F32)
        shift = keep.tile([P, ND], F32)
        for d in range(ND):
            nc.vector.tensor_scalar_mul(
                out=pair_gain[:, d : d + 1], in0=w_rows[:, d : d + 1], scalar1=PAIR_SIGN[d]
            )
            nc.vector.tensor_scalar_mul(
                out=half_gain[:, d : d + 1], in0=w_rows[:, d : d + 1], scalar1=HALF_SIGN[d]
            )
        nc.vector.tensor_copy(out=shift[:], in_=bias_rows[:])

        WIDE = TILES * NJ

        def flip_mask(st):
            m_words = st["m_raw"][:].rearrange("p h k -> p (h k)").bitcast(F32)
            m_by_u = m_words.rearrange("p (h q u) -> p h u q", h=TILES, u=PACK // 2)
            m_flip = flipped_mask.tile([P, TILES, PACK // 2, I_TILE], F32)
            for h in range(TILES):
                for u in range(PACK // 2):
                    nc.tensor.transpose(m_flip[:, h, u, :], m_by_u[:, h, u, :], identity[:])
            st["m_flip"] = m_flip

        def group_mask(st):
            m_grouped = front.tile([P, TILES, GROUPED], BF16)
            nc.scalar.copy(
                out=m_grouped[:].rearrange("p h c -> p (h c)").bitcast(F32).rearrange(
                    "p (h i u) -> p h i u", h=TILES, u=PACK // 2
                ),
                in_=st["m_flip"][:].rearrange("p h u i -> p h i u"),
            )
            st["m_grouped"] = m_grouped

        def split_channels(st, h):
            if h == 0:
                st["a_split"] = front.tile([P, TILES, 2, NK], BF16, name="a_split")
            k_by_half = st["a_raw"][:, h, :].rearrange("p (q u v d) -> p d u q v", u=2, v=2, d=ND)
            for e in range(2):
                nc.gpsimd.tensor_scalar(
                    out=st["a_split"][:, h, e, :].rearrange("p (u q v) -> p u q v", u=2, v=2),
                    in0=k_by_half[:, 2 + e],
                    scalar1=1.0, scalar2=0.0, op0=ALU.mult, op1=ALU.add,
                )

        def flip_split(st, part):
            words = st["a_split"][:].rearrange("p h e k -> p (h e k)").bitcast(F32)
            a_flip = flipped.tile([P, PACK * I_TILE], F32, name="a_flip")
            for eu in range(4):
                first = (part // 2 * 4 + eu) * P
                nc.tensor.transpose(
                    a_flip[:, eu * I_TILE : (eu + 1) * I_TILE], words[:, first : first + P], identity[:]
                )
            st["a_flip", part] = a_flip

        def flip_pair(st, part):
            h, pair = divmod(part, ND // 2)
            if pair == 1:
                return flip_split(st, part)
            a_words = st["a_raw"][:].rearrange("p h c -> p (h c)").bitcast(F32)
            a_by_pair = a_words.rearrange("p (h q t n) -> p h n t q", h=TILES, t=PACK, n=ND // 2)
            a_flip = flipped.tile([P, PACK * I_TILE], F32)
            for t in range(PACK):
                nc.tensor.transpose(
                    a_flip[:, t * I_TILE : (t + 1) * I_TILE], a_by_pair[:, h, pair, t, :], identity[:]
                )
            st["a_flip", part] = a_flip

        def mask_pair(st, part):
            h, pair = divmod(part, ND // 2)
            if part == 0:
                st["a_grouped"] = front.tile([P, TILES, ND, GROUPED], BF16, name="a_grouped", align_bytes=64)
            if pair == 1:
                nc.vector.tensor_tensor(
                    out=st["a_grouped"][:, h, 2:4, :].rearrange("p e (i u v) -> p i e u v", u=2, v=2),
                    in0=st["a_flip", part][:].bitcast(BF16).rearrange("p (e u i v) -> p i e u v", e=2, u=2, v=2),
                    in1=st["m_grouped"][:, h, :].rearrange("p (i u v) -> p i u v", u=2, v=2).unsqueeze(2).to_broadcast(
                        [P, I_TILE, 2, 2, 2]
                    ),
                    op=ALU.mult,
                )
                return
            nc.vector.tensor_tensor(
                out=st["a_grouped"][:, h, 2 * pair : 2 * pair + 2, :].rearrange("p e (i t) -> p e i t", t=PACK),
                in0=st["a_flip", part][:].bitcast(BF16).rearrange("p (t i e) -> p e i t", t=PACK, e=2),
                in1=st["m_grouped"][:, h, :].rearrange("p (i t) -> p i t", t=PACK).unsqueeze(1).to_broadcast(
                    [P, 2, I_TILE, PACK]
                ),
                op=ALU.mult,
            )

        def quantise(st):
            a_codes = front.tile([P, TILES, ND, I_TILE], U32, align_bytes=64)
            a_scales = front.tile([P, TILES, ND, I_TILE], U8, align_bytes=64)
            nc.vector.quantize_mx(
                out=a_codes[:].rearrange("p h d i -> p (h d i)").bitcast(FP8X4),
                scales=a_scales[:].rearrange("p h d i -> p (h d i)"),
                in_=st["a_grouped"][:].rearrange("p h d c -> p (h d c)"),
            )
            st["a_codes"], st["a_scales"] = a_codes, a_scales

        def multiply(st):
            for n, channels in enumerate(((0, 1), (2, 3), (0, 1, 2, 3))):
                acc = sums.tile([P, TILES, NJ], F32)
                st["c", n] = acc
                signs = HALF_SIGN if n == 2 else PAIR_SIGN
                for h in range(TILES):
                    for d in channels:
                        sign = PLUS if signs[d] > 0 else MINUS
                        nc.tensor.matmul_mx(
                            out=acc[:, h, :],
                            lhsT=st["a_codes"][:, h, d, :].bitcast(FP8X4),
                            lhsT_scale=st["a_scales"][:, h, d, :],
                            rhs=b_codes[:, sign, d, :].bitcast(FP8X4),
                            rhs_scale=b_scales[:, sign, d, :],
                            start=(d == channels[0]),
                            stop=(d == channels[-1]),
                        )

        def square(st, n):
            if n == 0:
                st["squares"] = norm.tile([P, 3, WIDE], F32, name="squares")
            nc.scalar.activation(
                out=st["squares"][:, n, :], in_=st["c", n][:].rearrange("p h j -> p (h j)"),
                func=ACT.Square, scale=SHARE[n],
            )

        def add_pair_squares(st):
            pair_squares = norm.tile([P, WIDE], F32)
            nc.gpsimd.tensor_tensor(
                out=pair_squares[:], in0=st["squares"][:, 0, :], in1=st["squares"][:, 1, :], op=ALU.add
            )
            st["pair_squares"] = pair_squares

        def add_third_square(st):
            var = norm.tile([P, WIDE], F32)
            nc.gpsimd.tensor_tensor(
                out=var[:], in0=st["pair_squares"][:], in1=st["squares"][:, 2, :], op=ALU.add
            )
            st["var"] = var

        def invert(st):
            rstd = norm.tile([P, WIDE], F32)
            nc.scalar.activation(
                out=rstd[:], in_=st["var"][:], func=ACT.Abs_reciprocal_sqrt, scale=1.0, bias=EPS
            )
            st["rstd"] = rstd

        def normalise(st):
            normed = norm.tile([P, 3, WIDE], F32)
            for n in range(3):
                nc.vector.scalar_tensor_tensor(
                    out=normed[:, n, :], in0=st["c", n][:].rearrange("p h j -> p (h j)"),
                    scalar=FACTOR[n], in1=st["rstd"][:], op0=ALU.mult, op1=ALU.mult,
                )
            st["normed"] = normed

        def pair_part(st, d):
            if d == 0:
                st["pair_part"] = norm.tile([P, ND, WIDE], F32, name="pair_part")
            nc.scalar.activation(
                out=st["pair_part"][:, d, :], in_=st["normed"][:, d // 2, :], func=ACT.Identity,
                scale=pair_gain[:, d : d + 1],
            )

        def half_part(st, d):
            if d == 0:
                st["half_part"] = norm.tile([P, ND, WIDE], F32, name="half_part")
            nc.scalar.activation(
                out=st["half_part"][:, d, :], in_=st["normed"][:, 2, :], func=ACT.Identity,
                scale=half_gain[:, d : d + 1], bias=shift[:, d : d + 1],
            )

        def finish(st, engine, h, first, count):
            if (h, first) == (0, 0):
                st["y"] = norm.tile([P, TILES, NJ * ND], F32, name="y")
            cols = slice(h * NJ + first, h * NJ + first + count)
            engine.tensor_tensor(
                out=st["y"][:, h, first * ND : (first + count) * ND].rearrange(
                    "p (g n d) -> p g d n", n=2, d=ND
                ),
                in0=st["pair_part"][:, :, cols].rearrange("p d (g n) -> p g d n", n=2),
                in1=st["half_part"][:, :, cols].rearrange("p d (g n) -> p g d n", n=2),
                op=ALU.add,
            )

        def store(r, st, h):
            nc.sync.dma_start(out=out_tiles[r, h], in_=st["y"][:, h, :])

        state = [{} for x in range(ROUNDS)]

        def load(r):
            if r < ROUNDS:
                state[r]["a_raw"], state[r]["m_raw"] = load_round(r) if r > 0 else first_raw

        with tc.manual_schedule():
            for r in range(3):
                load(r)
            for h in range(TILES):
                split_channels(state[0], h)
            flip_mask(state[0])
            group_mask(state[0])
            for part in range(3):
                flip_pair(state[0], part)
            for h in range(TILES):
                split_channels(state[1], h)
            for s in range(ROUNDS + 3):
                far, ahead, now, mid, back, end = [
                    state[x] if 0 <= x < ROUNDS else None for x in (s + 2, s + 1, s, s - 1, s - 2, s - 3)
                ]
                load(s + 3)
                if mid:
                    multiply(mid)
                if now:
                    flip_pair(now, 3)
                if ahead:
                    flip_mask(ahead)
                if end:
                    for h in range(TILES):
                        finish(end, nc.vector, h, 0, NJ)
                        store(s - 3, end, h)
                if mid:
                    square(mid, 0)
                    square(mid, 1)
                    add_pair_squares(mid)
                if back:
                    pair_part(back, 0)
                if mid:
                    square(mid, 2)
                    add_third_square(mid)
                if far:
                    for h in range(TILES):
                        split_channels(far, h)
                if back:
                    pair_part(back, 1)
                    pair_part(back, 2)
                if mid:
                    invert(mid)
                for part in range(4):
                    if now:
                        mask_pair(now, part)
                    if ahead and part < 3:
                        flip_pair(ahead, part)
                if ahead:
                    group_mask(ahead)
                if back:
                    pair_part(back, 3)
                    for d in range(ND):
                        half_part(back, d)
                if now:
                    quantise(now)
                if mid:
                    normalise(mid)
